import numpy as np
import ml_dtypes

BF16 = ml_dtypes.bfloat16


def bf(x):
    return np.asarray(x, np.float32).astype(BF16)


def f32(x):
    return np.asarray(x, np.float32)


def f64(x):
    return np.asarray(x).astype(np.float64)


def striped(idx):
    return np.tile(idx.reshape(-1, 16).T, (8, 1))


C, K, D, S, N, R = 1024, 4, 256, 1024, 512, 8
EPS = 1e-12
NOISE = 1.4


def l2n(v):
    n = np.sqrt(np.sum(v * v, axis=-1, keepdims=True))
    return v / np.maximum(n, EPS)


def setup_inputs():
    basis = np.random.standard_normal((R, D))
    codes = l2n(np.random.standard_normal((N, R)) @ basis + NOISE * np.random.standard_normal((N, D)))
    centroids = 0.1 * (np.random.standard_normal((C, K, R)) @ basis + NOISE * np.random.standard_normal((C, K, D)))
    return {"base": f32(np.random.standard_normal((C, S))), "codes": bf(codes.T), "centroids": f32(centroids), "offs": striped(np.random.permutation(S)[:N])}


def reference(base, codes, centroids, offs):
    idx = offs[:16].T.reshape(-1)
    cn = l2n(f64(centroids))
    sim = (cn.reshape(C * K, D) @ f64(codes)).reshape(C, K, N)
    m = np.max(sim, axis=1)
    out = f64(base).copy()
    out[:, idx] = 1.0 + (-m)
    return out

@@ -1,0 +1,89 @@
+import concourse.mybir as mybir
+from concourse.masks import make_identity
+
+F32 = mybir.dt.float32
+BF16 = mybir.dt.bfloat16
+U16 = mybir.dt.uint16
+SQUARE = mybir.ActivationFunctionType.Square
+ADD = mybir.AluOpType.add
+
+P = 128
+C, K, D, S, N = 1024, 4, 256, 1024, 512
+BLOCKS = C // P
+HALVES = D // P
+EPS = 1e-12
+
+FLOPS = 2 * C * K * D * N
+
+
+def tile_osrsaf_trinet_kernel(tc, base, codes, centroids, offs, out):
+    nc = tc.nc
+    base_blocks = base.rearrange("(b p) s -> b p s", p=P)
+    out_blocks = out.rearrange("(b p) s -> b p s", p=P)
+    centroid_blocks = centroids.rearrange("(b p) k d -> b p k d", p=P)
+
+    with (
+        tc.tile_pool(name="held", bufs=1) as held,
+        tc.tile_pool(name="loads", bufs=3) as loads,
+        tc.tile_pool(name="windows", bufs=4) as windows,
+        tc.tile_pool(name="work", bufs=2) as work,
+        tc.psum_pool(name="flip_banks", bufs=2) as flip_banks,
+        tc.psum_pool(name="sim_banks", bufs=6) as sim_banks,
+    ):
+        offsets = held.tile([P, N // 16], U16, name="offsets")
+        nc.sync.dma_start(offsets[:], offs)
+        codes_sb = held.tile([P, HALVES, N], BF16, name="codes_sb")
+        nc.sync.dma_start(codes_sb[:], codes.rearrange("(h p) j -> p h j", p=P))
+        identity = held.tile([P, P], BF16, name="identity")
+        make_identity(nc, identity[:])
+        ones = held.tile([P, N], F32, name="ones")
+        nc.gpsimd.memset(ones[:], 1.0)
+
+        def normalise_and_flip(b):
+            raw = loads.tile([P, K, D], F32, name="raw")
+            nc.sync.dma_start(raw[:], centroid_blocks[b, :, :, :])
+            sumsq = work.tile([P, K], F32, name="sumsq")
+            squares = work.tile([P, D], F32, name="squares")
+            for k in range(K):
+                nc.scalar.activation(squares[:], raw[:, k, :], SQUARE, accum_out=sumsq[:, k : k + 1])
+            inverse = work.tile([P, K], F32, name="inverse")
+            nc.vector.tensor_scalar_max(inverse[:], sumsq[:], EPS * EPS)
+            nc.scalar.sqrt(inverse[:], inverse[:])
+            nc.vector.reciprocal(inverse[:], inverse[:])
+            cn = work.tile([P, K, D], BF16, name="cn")
+            for k in range(K):
+                nc.gpsimd.tensor_scalar_mul(cn[:, k, :], raw[:, k, :], inverse[:, k : k + 1])
+            flipped = flip_banks.tile([P, K, HALVES, P], BF16, name="flipped")
+            for k in range(K):
+                for h in range(HALVES):
+                    nc.tensor.transpose(flipped[:, k, h, :], cn[:, k, h * P : (h + 1) * P], identity[:])
+            cn_t = work.tile([P, K, HALVES, P], BF16, name="cn_t")
+            nc.scalar.copy(cn_t[:], flipped[:])
+            return cn_t
+
+        def score_and_place(b, cn_t):
+            window = windows.tile([P, S], F32, name="window")
+            nc.sync.dma_start(window[:], base_blocks[b, :, :])
+            sims = []
+            for k in range(K):
+                sim = sim_banks.tile([P, N], F32, name="sim")
+                for h in range(HALVES):
+                    nc.tensor.matmul(
+                        sim[:], cn_t[:, k, h, :], codes_sb[:, h, :], start=(h == 0), stop=(h == HALVES - 1)
+                    )
+                sims.append(sim)
+            best = work.tile([P, N], F32, name="best")
+            nc.scalar.copy(best[:], sims[0][:])
+            for k in range(1, K):
+                nc.vector.tensor_max(best[:], best[:], sims[k][:])
+            negated = work.tile([P, N], F32, name="negated")
+            nc.scalar.mul(negated[:], best[:], -1.0)
+            nc.vector.tensor_tensor(window[:].indirect(offsets[:]), ones[:], negated[:], ADD)
+            nc.sync.dma_start(out_blocks[b, :, :], window[:])
+
+        cn_t_next = normalise_and_flip(0)
+        for b in range(BLOCKS):
+            cn_t = cn_t_next
+            if b + 1 < BLOCKS:
+                cn_t_next = normalise_and_flip(b + 1)
+            score_and_place(b, cn_t)

@@ -5,6 +5,8 @@ F32 = mybir.dt.float32
 BF16 = mybir.dt.bfloat16
 U16 = mybir.dt.uint16
 SQUARE = mybir.ActivationFunctionType.Square
+RSQRT = mybir.ActivationFunctionType.Abs_reciprocal_sqrt
+COPY = mybir.ActivationFunctionType.Copy
 ADD = mybir.AluOpType.add
 
 P = 128
@@ -24,8 +26,7 @@ def tile_osrsaf_trinet_kernel(tc, base, codes, centroids, offs, out):
 
     with (
         tc.tile_pool(name="held", bufs=1) as held,
-        tc.tile_pool(name="loads", bufs=3) as loads,
-        tc.tile_pool(name="windows", bufs=4) as windows,
+        tc.tile_pool(name="inputs", bufs=BLOCKS) as inputs,
         tc.tile_pool(name="work", bufs=2) as work,
         tc.psum_pool(name="flip_banks", bufs=2) as flip_banks,
         tc.psum_pool(name="sim_banks", bufs=6) as sim_banks,
@@ -33,26 +34,35 @@ def tile_osrsaf_trinet_kernel(tc, base, codes, centroids, offs, out):
         offsets = held.tile([P, N // 16], U16, name="offsets")
         nc.sync.dma_start(offsets[:], offs)
         codes_sb = held.tile([P, HALVES, N], BF16, name="codes_sb")
-        nc.sync.dma_start(codes_sb[:], codes.rearrange("(h p) j -> p h j", p=P))
+        nc.scalar.dma_start(codes_sb[:], codes.rearrange("(h p) j -> p h j", p=P))
+        raws = [inputs.tile([P, K, D], F32, name="raw") for b in range(BLOCKS)]
+        windows = [inputs.tile([P, S], F32, name="window") for b in range(BLOCKS)]
+        for b in range(BLOCKS + 3):
+            if b < BLOCKS:
+                nc.sync.dma_start(raws[b][:], centroid_blocks[b, :, :, :])
+            if b >= 3:
+                nc.sync.dma_start(windows[b - 3][:], base_blocks[b - 3, :, :])
         identity = held.tile([P, P], BF16, name="identity")
         make_identity(nc, identity[:])
         ones = held.tile([P, N], F32, name="ones")
         nc.gpsimd.memset(ones[:], 1.0)
 
-        def normalise_and_flip(b):
-            raw = loads.tile([P, K, D], F32, name="raw")
-            nc.sync.dma_start(raw[:], centroid_blocks[b, :, :, :])
+        def normalise(b):
+            raw = raws[b]
             sumsq = work.tile([P, K], F32, name="sumsq")
             squares = work.tile([P, D], F32, name="squares")
             for k in range(K):
                 nc.scalar.activation(squares[:], raw[:, k, :], SQUARE, accum_out=sumsq[:, k : k + 1])
+            clamped = work.tile([P, K], F32, name="clamped")
+            nc.gpsimd.tensor_scalar_max(clamped[:], sumsq[:], EPS * EPS)
             inverse = work.tile([P, K], F32, name="inverse")
-            nc.vector.tensor_scalar_max(inverse[:], sumsq[:], EPS * EPS)
-            nc.scalar.sqrt(inverse[:], inverse[:])
-            nc.vector.reciprocal(inverse[:], inverse[:])
+            nc.scalar.activation(inverse[:], clamped[:], RSQRT)
             cn = work.tile([P, K, D], BF16, name="cn")
             for k in range(K):
-                nc.gpsimd.tensor_scalar_mul(cn[:, k, :], raw[:, k, :], inverse[:, k : k + 1])
+                nc.scalar.activation(cn[:, k, :], raw[:, k, :], COPY, scale=inverse[:, k : k + 1])
+            return cn
+
+        def flip(cn):
             flipped = flip_banks.tile([P, K, HALVES, P], BF16, name="flipped")
             for k in range(K):
                 for h in range(HALVES):
@@ -61,9 +71,7 @@ def tile_osrsaf_trinet_kernel(tc, base, codes, centroids, offs, out):
             nc.scalar.copy(cn_t[:], flipped[:])
             return cn_t
 
-        def score_and_place(b, cn_t):
-            window = windows.tile([P, S], F32, name="window")
-            nc.sync.dma_start(window[:], base_blocks[b, :, :])
+        def score(cn_t):
             sims = []
             for k in range(K):
                 sim = sim_banks.tile([P, N], F32, name="sim")
@@ -77,13 +85,20 @@ def tile_osrsaf_trinet_kernel(tc, base, codes, centroids, offs, out):
             for k in range(1, K):
                 nc.vector.tensor_max(best[:], best[:], sims[k][:])
             negated = work.tile([P, N], F32, name="negated")
-            nc.scalar.mul(negated[:], best[:], -1.0)
-            nc.vector.tensor_tensor(window[:].indirect(offsets[:]), ones[:], negated[:], ADD)
-            nc.sync.dma_start(out_blocks[b, :, :], window[:])
+            nc.gpsimd.tensor_scalar_mul(negated[:], best[:], -1.0)
+            return negated
 
-        cn_t_next = normalise_and_flip(0)
-        for b in range(BLOCKS):
-            cn_t = cn_t_next
-            if b + 1 < BLOCKS:
-                cn_t_next = normalise_and_flip(b + 1)
-            score_and_place(b, cn_t)
+        def place(b, negated):
+            nc.vector.tensor_tensor(windows[b][:].indirect(offsets[:]), ones[:], negated[:], ADD)
+            nc.sync.dma_start(out_blocks[b, :, :], windows[b][:])
+
+        cns, cn_ts, negateds = {}, {}, {}
+        for step in range(BLOCKS + 3):
+            if 0 <= step - 2 < BLOCKS:
+                negateds[step - 2] = score(cn_ts[step - 2])
+            if 0 <= step - 3 < BLOCKS:
+                place(step - 3, negateds[step - 3])
+            if 0 <= step - 1 < BLOCKS:
+                cn_ts[step - 1] = flip(cns[step - 1])
+            if step < BLOCKS:
+                cns[step] = normalise(step)

@@ -5,6 +5,7 @@ F32 = mybir.dt.float32
 BF16 = mybir.dt.bfloat16
 U16 = mybir.dt.uint16
 SQUARE = mybir.ActivationFunctionType.Square
+RELU = mybir.ActivationFunctionType.Relu
 RSQRT = mybir.ActivationFunctionType.Abs_reciprocal_sqrt
 COPY = mybir.ActivationFunctionType.Copy
 ADD = mybir.AluOpType.add
@@ -13,6 +14,7 @@ P = 128
 C, K, D, S, N = 1024, 4, 256, 1024, 512
 BLOCKS = C // P
 HALVES = D // P
+PAIR = 2
 EPS = 1e-12
 
 FLOPS = 2 * C * K * D * N
@@ -31,44 +33,54 @@ def tile_osrsaf_trinet_kernel(tc, base, codes, centroids, offs, out):
         tc.psum_pool(name="flip_banks", bufs=2) as flip_banks,
         tc.psum_pool(name="sim_banks", bufs=6) as sim_banks,
     ):
-        offsets = held.tile([P, N // 16], U16, name="offsets")
-        nc.sync.dma_start(offsets[:], offs)
-        codes_sb = held.tile([P, HALVES, N], BF16, name="codes_sb")
-        nc.scalar.dma_start(codes_sb[:], codes.rearrange("(h p) j -> p h j", p=P))
         raws = [inputs.tile([P, K, D], F32, name="raw") for b in range(BLOCKS)]
         windows = [inputs.tile([P, S], F32, name="window") for b in range(BLOCKS)]
-        for b in range(BLOCKS + 3):
-            if b < BLOCKS:
-                nc.sync.dma_start(raws[b][:], centroid_blocks[b, :, :, :])
-            if b >= 3:
-                nc.sync.dma_start(windows[b - 3][:], base_blocks[b - 3, :, :])
+        codes_sb = held.tile([P, HALVES, N], BF16, name="codes_sb")
+        offsets = held.tile([P, N // 16], U16, name="offsets")
+
+        def load_centroids(b):
+            for k in range(K):
+                nc.sync.dma_start(raws[b][:, k, :], centroid_blocks[b, :, k, :])
+
+        load_centroids(0)
+        nc.sync.dma_start(codes_sb[:], codes.rearrange("(h p) j -> p h j", p=P))
+        nc.sync.dma_start(offsets[:], offs)
+        for b in range(BLOCKS):
+            if b + 1 < BLOCKS:
+                load_centroids(b + 1)
+            nc.sync.dma_start(windows[b][:], base_blocks[b, :, :])
+
         identity = held.tile([P, P], BF16, name="identity")
         make_identity(nc, identity[:])
         ones = held.tile([P, N], F32, name="ones")
         nc.gpsimd.memset(ones[:], 1.0)
+        floor = held.tile([P, 1], F32, name="floor")
+        nc.gpsimd.memset(floor[:], EPS * EPS)
+        minus_floor = held.tile([P, 1], F32, name="minus_floor")
+        nc.gpsimd.memset(minus_floor[:], -EPS * EPS)
 
         def normalise(b):
-            raw = raws[b]
             sumsq = work.tile([P, K], F32, name="sumsq")
             squares = work.tile([P, D], F32, name="squares")
             for k in range(K):
-                nc.scalar.activation(squares[:], raw[:, k, :], SQUARE, accum_out=sumsq[:, k : k + 1])
-            clamped = work.tile([P, K], F32, name="clamped")
-            nc.gpsimd.tensor_scalar_max(clamped[:], sumsq[:], EPS * EPS)
+                nc.scalar.activation(squares[:], raws[b][:, k, :], SQUARE, accum_out=sumsq[:, k : k + 1])
+            excess = work.tile([P, K], F32, name="excess")
+            nc.scalar.activation(excess[:], sumsq[:], RELU, bias=minus_floor[:])
             inverse = work.tile([P, K], F32, name="inverse")
-            nc.scalar.activation(inverse[:], clamped[:], RSQRT)
+            nc.scalar.activation(inverse[:], excess[:], RSQRT, bias=floor[:])
             cn = work.tile([P, K, D], BF16, name="cn")
             for k in range(K):
-                nc.scalar.activation(cn[:, k, :], raw[:, k, :], COPY, scale=inverse[:, k : k + 1])
+                nc.scalar.activation(cn[:, k, :], raws[b][:, k, :], COPY, scale=inverse[:, k : k + 1])
             return cn
 
         def flip(cn):
-            flipped = flip_banks.tile([P, K, HALVES, P], BF16, name="flipped")
-            for k in range(K):
-                for h in range(HALVES):
-                    nc.tensor.transpose(flipped[:, k, h, :], cn[:, k, h * P : (h + 1) * P], identity[:])
             cn_t = work.tile([P, K, HALVES, P], BF16, name="cn_t")
-            nc.scalar.copy(cn_t[:], flipped[:])
+            for first in range(0, K, PAIR):
+                flipped = flip_banks.tile([P, PAIR, HALVES, P], BF16, name="flipped")
+                for i in range(PAIR):
+                    for h in range(HALVES):
+                        nc.tensor.transpose(flipped[:, i, h, :], cn[:, first + i, h * P : (h + 1) * P], identity[:])
+                nc.scalar.copy(cn_t[:, first : first + PAIR, :, :], flipped[:])
             return cn_t
 
         def score(cn_t):
@@ -82,23 +94,18 @@ def tile_osrsaf_trinet_kernel(tc, base, codes, centroids, offs, out):
                 sims.append(sim)
             best = work.tile([P, N], F32, name="best")
             nc.scalar.copy(best[:], sims[0][:])
+            sides = [slice(0, N // 2), slice(N // 2, N)]
             for k in range(1, K):
-                nc.vector.tensor_max(best[:], best[:], sims[k][:])
+                for side in sides:
+                    nc.vector.tensor_max(best[:, side], best[:, side], sims[k][:, side])
             negated = work.tile([P, N], F32, name="negated")
-            nc.gpsimd.tensor_scalar_mul(negated[:], best[:], -1.0)
+            for side in sides:
+                nc.vector.tensor_scalar_mul(negated[:, side], best[:, side], -1.0)
             return negated
 
         def place(b, negated):
             nc.vector.tensor_tensor(windows[b][:].indirect(offsets[:]), ones[:], negated[:], ADD)
             nc.sync.dma_start(out_blocks[b, :, :], windows[b][:])
 
-        cns, cn_ts, negateds = {}, {}, {}
-        for step in range(BLOCKS + 3):
-            if 0 <= step - 2 < BLOCKS:
-                negateds[step - 2] = score(cn_ts[step - 2])
-            if 0 <= step - 3 < BLOCKS:
-                place(step - 3, negateds[step - 3])
-            if 0 <= step - 1 < BLOCKS:
-                cn_ts[step - 1] = flip(cns[step - 1])
-            if step < BLOCKS:
-                cns[step] = normalise(step)
+        for b in range(BLOCKS):
+            place(b, score(flip(normalise(b))))

@@ -94,7 +94,7 @@ def tile_osrsaf_trinet_kernel(tc, base, codes, centroids, offs, out):
                 sims.append(sim)
             best = work.tile([P, N], F32, name="best")
             nc.scalar.copy(best[:], sims[0][:])
-            sides = [slice(0, N // 2), slice(N // 2, N)]
+            sides = [slice(q, q + N // 4) for q in range(0, N, N // 4)]
             for k in range(1, K):
                 for side in sides:
                     nc.vector.tensor_max(best[:, side], best[:, side], sims[k][:, side])

@@ -14,7 +14,7 @@ P = 128
 C, K, D, S, N = 1024, 4, 256, 1024, 512
 BLOCKS = C // P
 HALVES = D // P
-PAIR = 2
+TWINS = 2
 EPS = 1e-12
 
 FLOPS = 2 * C * K * D * N
@@ -29,7 +29,7 @@ def tile_osrsaf_trinet_kernel(tc, base, codes, centroids, offs, out):
     with (
         tc.tile_pool(name="held", bufs=1) as held,
         tc.tile_pool(name="inputs", bufs=BLOCKS) as inputs,
-        tc.tile_pool(name="work", bufs=2) as work,
+        tc.tile_pool(name="work", bufs=4) as work,
         tc.psum_pool(name="flip_banks", bufs=2) as flip_banks,
         tc.psum_pool(name="sim_banks", bufs=6) as sim_banks,
     ):
@@ -37,18 +37,17 @@ def tile_osrsaf_trinet_kernel(tc, base, codes, centroids, offs, out):
         windows = [inputs.tile([P, S], F32, name="window") for b in range(BLOCKS)]
         codes_sb = held.tile([P, HALVES, N], BF16, name="codes_sb")
         offsets = held.tile([P, N // 16], U16, name="offsets")
-
-        def load_centroids(b):
+        for first in range(0, BLOCKS, TWINS):
+            twins = range(first, first + TWINS)
             for k in range(K):
-                nc.sync.dma_start(raws[b][:, k, :], centroid_blocks[b, :, k, :])
-
-        load_centroids(0)
-        nc.sync.dma_start(codes_sb[:], codes.rearrange("(h p) j -> p h j", p=P))
-        nc.sync.dma_start(offsets[:], offs)
-        for b in range(BLOCKS):
-            if b + 1 < BLOCKS:
-                load_centroids(b + 1)
-            nc.sync.dma_start(windows[b][:], base_blocks[b, :, :])
+                for b in twins:
+                    nc.sync.dma_start(raws[b][:, k, :], centroid_blocks[b, :, k, :])
+                if first == 0 and k == 0:
+                    nc.sync.dma_start(codes_sb[:], codes.rearrange("(h p) j -> p h j", p=P))
+            if first == 0:
+                nc.sync.dma_start(offsets[:], offs)
+            for b in twins:
+                nc.sync.dma_start(windows[b][:], base_blocks[b, :, :])
 
         identity = held.tile([P, P], BF16, name="identity")
         make_identity(nc, identity[:])
@@ -59,53 +58,50 @@ def tile_osrsaf_trinet_kernel(tc, base, codes, centroids, offs, out):
         minus_floor = held.tile([P, 1], F32, name="minus_floor")
         nc.gpsimd.memset(minus_floor[:], -EPS * EPS)
 
-        def normalise(b):
-            sumsq = work.tile([P, K], F32, name="sumsq")
+        def normalise_and_flip(twins, k):
+            sumsq = work.tile([P, TWINS], F32, name="sumsq")
             squares = work.tile([P, D], F32, name="squares")
-            for k in range(K):
-                nc.scalar.activation(squares[:], raws[b][:, k, :], SQUARE, accum_out=sumsq[:, k : k + 1])
-            excess = work.tile([P, K], F32, name="excess")
+            for i, b in enumerate(twins):
+                nc.scalar.activation(squares[:], raws[b][:, k, :], SQUARE, accum_out=sumsq[:, i : i + 1])
+            excess = work.tile([P, TWINS], F32, name="excess")
             nc.scalar.activation(excess[:], sumsq[:], RELU, bias=minus_floor[:])
-            inverse = work.tile([P, K], F32, name="inverse")
+            inverse = work.tile([P, TWINS], F32, name="inverse")
             nc.scalar.activation(inverse[:], excess[:], RSQRT, bias=floor[:])
-            cn = work.tile([P, K, D], BF16, name="cn")
-            for k in range(K):
-                nc.scalar.activation(cn[:, k, :], raws[b][:, k, :], COPY, scale=inverse[:, k : k + 1])
-            return cn
-
-        def flip(cn):
-            cn_t = work.tile([P, K, HALVES, P], BF16, name="cn_t")
-            for first in range(0, K, PAIR):
-                flipped = flip_banks.tile([P, PAIR, HALVES, P], BF16, name="flipped")
-                for i in range(PAIR):
-                    for h in range(HALVES):
-                        nc.tensor.transpose(flipped[:, i, h, :], cn[:, first + i, h * P : (h + 1) * P], identity[:])
-                nc.scalar.copy(cn_t[:, first : first + PAIR, :, :], flipped[:])
+            cn = work.tile([P, TWINS, D], BF16, name="cn")
+            for i, b in enumerate(twins):
+                nc.scalar.activation(cn[:, i, :], raws[b][:, k, :], COPY, scale=inverse[:, i : i + 1])
+            flipped = flip_banks.tile([P, TWINS, HALVES, P], BF16, name="flipped")
+            for i in range(TWINS):
+                for h in range(HALVES):
+                    nc.tensor.transpose(flipped[:, i, h, :], cn[:, i, h * P : (h + 1) * P], identity[:])
+            cn_t = work.tile([P, TWINS, HALVES, P], BF16, name="cn_t")
+            nc.scalar.copy(cn_t[:], flipped[:])
             return cn_t
 
-        def score(cn_t):
+        def similarities(cn_t):
             sims = []
-            for k in range(K):
+            for i in range(TWINS):
                 sim = sim_banks.tile([P, N], F32, name="sim")
                 for h in range(HALVES):
                     nc.tensor.matmul(
-                        sim[:], cn_t[:, k, h, :], codes_sb[:, h, :], start=(h == 0), stop=(h == HALVES - 1)
+                        sim[:], cn_t[:, i, h, :], codes_sb[:, h, :], start=(h == 0), stop=(h == HALVES - 1)
                     )
                 sims.append(sim)
-            best = work.tile([P, N], F32, name="best")
-            nc.scalar.copy(best[:], sims[0][:])
-            sides = [slice(q, q + N // 4) for q in range(0, N, N // 4)]
-            for k in range(1, K):
-                for side in sides:
-                    nc.vector.tensor_max(best[:, side], best[:, side], sims[k][:, side])
-            negated = work.tile([P, N], F32, name="negated")
-            for side in sides:
-                nc.vector.tensor_scalar_mul(negated[:, side], best[:, side], -1.0)
-            return negated
+            return sims
 
-        def place(b, negated):
-            nc.vector.tensor_tensor(windows[b][:].indirect(offsets[:]), ones[:], negated[:], ADD)
-            nc.sync.dma_start(out_blocks[b, :, :], windows[b][:])
-
-        for b in range(BLOCKS):
-            place(b, score(flip(normalise(b))))
+        for first in range(0, BLOCKS, TWINS):
+            twins = range(first, first + TWINS)
+            bests = [work.tile([P, N], F32, name="best") for b in twins]
+            for k in range(K):
+                sims = similarities(normalise_and_flip(twins, k))
+                for best, sim in zip(bests, sims):
+                    if k == 0:
+                        nc.scalar.copy(best[:], sim[:])
+                    else:
+                        nc.vector.tensor_max(best[:], best[:], sim[:])
+            negateds = [work.tile([P, N], F32, name="negated") for b in twins]
+            for best, negated in zip(bests, negateds):
+                nc.vector.tensor_scalar_mul(negated[:], best[:], -1.0)
+            for b, negated in zip(twins, negateds):
+                nc.vector.tensor_tensor(windows[b][:].indirect(offsets[:]), ones[:], negated[:], ADD)
+                nc.sync.dma_start(out_blocks[b, :, :], windows[b][:])

@@ -14,10 +14,11 @@ P = 128
 C, K, D, S, N = 1024, 4, 256, 1024, 512
 BLOCKS = C // P
 HALVES = D // P
-TWINS = 2
 EPS = 1e-12
 
 FLOPS = 2 * C * K * D * N
+PAIR = 2
+LEAD = 2
 
 
 def tile_osrsaf_trinet_kernel(tc, base, codes, centroids, offs, out):
@@ -29,7 +30,9 @@ def tile_osrsaf_trinet_kernel(tc, base, codes, centroids, offs, out):
     with (
         tc.tile_pool(name="held", bufs=1) as held,
         tc.tile_pool(name="inputs", bufs=BLOCKS) as inputs,
+        tc.tile_pool(name="lengths", bufs=2) as lengths,
         tc.tile_pool(name="work", bufs=4) as work,
+        tc.tile_pool(name="ahead", bufs=8) as ahead,
         tc.psum_pool(name="flip_banks", bufs=2) as flip_banks,
         tc.psum_pool(name="sim_banks", bufs=6) as sim_banks,
     ):
@@ -37,17 +40,15 @@ def tile_osrsaf_trinet_kernel(tc, base, codes, centroids, offs, out):
         windows = [inputs.tile([P, S], F32, name="window") for b in range(BLOCKS)]
         codes_sb = held.tile([P, HALVES, N], BF16, name="codes_sb")
         offsets = held.tile([P, N // 16], U16, name="offsets")
-        for first in range(0, BLOCKS, TWINS):
-            twins = range(first, first + TWINS)
+        for b in range(BLOCKS):
             for k in range(K):
-                for b in twins:
-                    nc.sync.dma_start(raws[b][:, k, :], centroid_blocks[b, :, k, :])
-                if first == 0 and k == 0:
-                    nc.sync.dma_start(codes_sb[:], codes.rearrange("(h p) j -> p h j", p=P))
-            if first == 0:
+                nc.sync.dma_start(raws[b][:, k, :], centroid_blocks[b, :, k, :])
+            if b == 0:
+                nc.sync.dma_start(codes_sb[:], codes.rearrange("(h p) j -> p h j", p=P))
                 nc.sync.dma_start(offsets[:], offs)
-            for b in twins:
-                nc.sync.dma_start(windows[b][:], base_blocks[b, :, :])
+            else:
+                nc.sync.dma_start(windows[b - 1][:], base_blocks[b - 1, :, :])
+        nc.sync.dma_start(windows[BLOCKS - 1][:], base_blocks[BLOCKS - 1, :, :])
 
         identity = held.tile([P, P], BF16, name="identity")
         make_identity(nc, identity[:])
@@ -58,50 +59,71 @@ def tile_osrsaf_trinet_kernel(tc, base, codes, centroids, offs, out):
         minus_floor = held.tile([P, 1], F32, name="minus_floor")
         nc.gpsimd.memset(minus_floor[:], -EPS * EPS)
 
-        def normalise_and_flip(twins, k):
-            sumsq = work.tile([P, TWINS], F32, name="sumsq")
-            squares = work.tile([P, D], F32, name="squares")
-            for i, b in enumerate(twins):
+        def scaled(b, result, values, factor):
+            if b == 0:
+                nc.vector.tensor_scalar_mul(result, values, factor)
+            else:
+                nc.scalar.activation(result, values, COPY, scale=factor)
+
+        def moved(b, result, values):
+            if b == 0:
+                nc.vector.tensor_copy(result, values)
+            else:
+                nc.scalar.copy(result, values)
+
+        def normalise_and_flip(b, pair):
+            steps = lengths.tile([P, 3, PAIR], F32, name="steps")
+            sumsq, excess, inverse = steps[:, 0, :], steps[:, 1, :], steps[:, 2, :]
+            for i, k in enumerate(pair):
+                squares = work.tile([P, D], F32, name="squares")
                 nc.scalar.activation(squares[:], raws[b][:, k, :], SQUARE, accum_out=sumsq[:, i : i + 1])
-            excess = work.tile([P, TWINS], F32, name="excess")
-            nc.scalar.activation(excess[:], sumsq[:], RELU, bias=minus_floor[:])
-            inverse = work.tile([P, TWINS], F32, name="inverse")
-            nc.scalar.activation(inverse[:], excess[:], RSQRT, bias=floor[:])
-            cn = work.tile([P, TWINS, D], BF16, name="cn")
-            for i, b in enumerate(twins):
-                nc.scalar.activation(cn[:, i, :], raws[b][:, k, :], COPY, scale=inverse[:, i : i + 1])
-            flipped = flip_banks.tile([P, TWINS, HALVES, P], BF16, name="flipped")
-            for i in range(TWINS):
+            nc.scalar.activation(excess, sumsq, RELU, bias=minus_floor[:])
+            nc.scalar.activation(inverse, excess, RSQRT, bias=floor[:])
+            cn = work.tile([P, PAIR, D], BF16, name="cn")
+            for i, k in enumerate(pair):
+                scaled(b, cn[:, i, :], raws[b][:, k, :], inverse[:, i : i + 1])
+            flipped = flip_banks.tile([P, PAIR, HALVES, P], BF16, name="flipped")
+            for i in range(PAIR):
                 for h in range(HALVES):
                     nc.tensor.transpose(flipped[:, i, h, :], cn[:, i, h * P : (h + 1) * P], identity[:])
-            cn_t = work.tile([P, TWINS, HALVES, P], BF16, name="cn_t")
-            nc.scalar.copy(cn_t[:], flipped[:])
+            cn_t = ahead.tile([P, PAIR, HALVES, P], BF16, name="cn_t")
+            moved(b, cn_t[:], flipped[:])
             return cn_t
 
-        def similarities(cn_t):
-            sims = []
-            for i in range(TWINS):
-                sim = sim_banks.tile([P, N], F32, name="sim")
-                for h in range(HALVES):
-                    nc.tensor.matmul(
-                        sim[:], cn_t[:, i, h, :], codes_sb[:, h, :], start=(h == 0), stop=(h == HALVES - 1)
-                    )
-                sims.append(sim)
-            return sims
+        cn_ts = []
 
-        for first in range(0, BLOCKS, TWINS):
-            twins = range(first, first + TWINS)
-            bests = [work.tile([P, N], F32, name="best") for b in twins]
-            for k in range(K):
-                sims = similarities(normalise_and_flip(twins, k))
-                for best, sim in zip(bests, sims):
-                    if k == 0:
-                        nc.scalar.copy(best[:], sim[:])
-                    else:
-                        nc.vector.tensor_max(best[:], best[:], sim[:])
-            negateds = [work.tile([P, N], F32, name="negated") for b in twins]
-            for best, negated in zip(bests, negateds):
-                nc.vector.tensor_scalar_mul(negated[:], best[:], -1.0)
-            for b, negated in zip(twins, negateds):
-                nc.vector.tensor_tensor(windows[b][:].indirect(offsets[:]), ones[:], negated[:], ADD)
-                nc.sync.dma_start(out_blocks[b, :, :], windows[b][:])
+        def normalise_block(b):
+            cn_ts.append([normalise_and_flip(b, range(first, first + PAIR)) for first in range(0, K, PAIR)])
+
+        def similarity(b, k):
+            sim = sim_banks.tile([P, N], F32, name="sim")
+            for h in range(HALVES):
+                nc.tensor.matmul(
+                    sim[:], cn_ts[b][k // PAIR][:, k % PAIR, h, :], codes_sb[:, h, :],
+                    start=(h == 0), stop=(h == HALVES - 1),
+                )
+            return sim
+
+        for b in range(LEAD):
+            normalise_block(b)
+        bests = []
+        negateds = []
+        for t in range(BLOCKS + 2):
+            if t < BLOCKS:
+                best = work.tile([P, N], F32, name="best")
+                bests.append(best)
+                moved(t, best[:], similarity(t, 0)[:])
+                nc.vector.tensor_max(best[:], best[:], similarity(t, 1)[:])
+            if 1 <= t <= BLOCKS:
+                nc.vector.tensor_max(bests[t - 1][:], bests[t - 1][:], similarity(t - 1, 3)[:])
+            if t < BLOCKS:
+                nc.vector.tensor_max(best[:], best[:], similarity(t, 2)[:])
+            if 1 <= t <= BLOCKS:
+                negated = work.tile([P, N], F32, name="negated")
+                negateds.append(negated)
+                nc.vector.tensor_scalar_mul(negated[:], bests[t - 1][:], -1.0)
+            if t >= 2:
+                nc.vector.tensor_tensor(windows[t - 2][:].indirect(offsets[:]), ones[:], negateds[t - 2][:], ADD)
+                nc.sync.dma_start(out_blocks[t - 2, :, :], windows[t - 2][:])
+            if t + LEAD < BLOCKS:
+                normalise_block(t + LEAD)

@@ -9,6 +9,7 @@ RELU = mybir.ActivationFunctionType.Relu
 RSQRT = mybir.ActivationFunctionType.Abs_reciprocal_sqrt
 COPY = mybir.ActivationFunctionType.Copy
 ADD = mybir.AluOpType.add
+MULT = mybir.AluOpType.mult
 
 P = 128
 C, K, D, S, N = 1024, 4, 256, 1024, 512
@@ -18,7 +19,8 @@ EPS = 1e-12
 
 FLOPS = 2 * C * K * D * N
 PAIR = 2
-LEAD = 2
+ALONE = 2
+HELPED = 1
 
 
 def tile_osrsaf_trinet_kernel(tc, base, codes, centroids, offs, out):
@@ -27,12 +29,17 @@ def tile_osrsaf_trinet_kernel(tc, base, codes, centroids, offs, out):
     out_blocks = out.rearrange("(b p) s -> b p s", p=P)
     centroid_blocks = centroids.rearrange("(b p) k d -> b p k d", p=P)
 
+    groups = [[b] for b in range(ALONE)] + [[b, b + 1] for b in range(ALONE, BLOCKS, 2)]
+    steps = []
+    for group in groups:
+        units = [(b, k) for k in range(K) for b in group]
+        steps.extend(units[i : i + PAIR] for i in range(0, len(units), PAIR))
+
     with (
         tc.tile_pool(name="held", bufs=1) as held,
         tc.tile_pool(name="inputs", bufs=BLOCKS) as inputs,
         tc.tile_pool(name="lengths", bufs=2) as lengths,
         tc.tile_pool(name="work", bufs=4) as work,
-        tc.tile_pool(name="ahead", bufs=8) as ahead,
         tc.psum_pool(name="flip_banks", bufs=2) as flip_banks,
         tc.psum_pool(name="sim_banks", bufs=6) as sim_banks,
     ):
@@ -40,15 +47,18 @@ def tile_osrsaf_trinet_kernel(tc, base, codes, centroids, offs, out):
         windows = [inputs.tile([P, S], F32, name="window") for b in range(BLOCKS)]
         codes_sb = held.tile([P, HALVES, N], BF16, name="codes_sb")
         offsets = held.tile([P, N // 16], U16, name="offsets")
-        for b in range(BLOCKS):
+        for g, group in enumerate(groups):
             for k in range(K):
-                nc.sync.dma_start(raws[b][:, k, :], centroid_blocks[b, :, k, :])
-            if b == 0:
+                for b in group:
+                    nc.sync.dma_start(raws[b][:, k, :], centroid_blocks[b, :, k, :])
+            if g == 0:
                 nc.sync.dma_start(codes_sb[:], codes.rearrange("(h p) j -> p h j", p=P))
                 nc.sync.dma_start(offsets[:], offs)
             else:
-                nc.sync.dma_start(windows[b - 1][:], base_blocks[b - 1, :, :])
-        nc.sync.dma_start(windows[BLOCKS - 1][:], base_blocks[BLOCKS - 1, :, :])
+                for b in groups[g - 1]:
+                    nc.sync.dma_start(windows[b][:], base_blocks[b, :, :])
+        for b in groups[-1]:
+            nc.sync.dma_start(windows[b][:], base_blocks[b, :, :])
 
         identity = held.tile([P, P], BF16, name="identity")
         make_identity(nc, identity[:])
@@ -60,70 +70,71 @@ def tile_osrsaf_trinet_kernel(tc, base, codes, centroids, offs, out):
         nc.gpsimd.memset(minus_floor[:], -EPS * EPS)
 
         def scaled(b, result, values, factor):
-            if b == 0:
+            if b < HELPED:
                 nc.vector.tensor_scalar_mul(result, values, factor)
             else:
                 nc.scalar.activation(result, values, COPY, scale=factor)
 
         def moved(b, result, values):
-            if b == 0:
+            if b < HELPED:
                 nc.vector.tensor_copy(result, values)
             else:
                 nc.scalar.copy(result, values)
 
-        def normalise_and_flip(b, pair):
-            steps = lengths.tile([P, 3, PAIR], F32, name="steps")
-            sumsq, excess, inverse = steps[:, 0, :], steps[:, 1, :], steps[:, 2, :]
-            for i, k in enumerate(pair):
+        def normalise_and_flip(step):
+            small = lengths.tile([P, 3, PAIR], F32, name="small")
+            sumsq, excess, inverse = small[:, 0, :], small[:, 1, :], small[:, 2, :]
+            for i, (b, k) in enumerate(step):
                 squares = work.tile([P, D], F32, name="squares")
-                nc.scalar.activation(squares[:], raws[b][:, k, :], SQUARE, accum_out=sumsq[:, i : i + 1])
+                if b < HELPED and k >= PAIR:
+                    nc.vector.scalar_tensor_tensor(
+                        squares[:], raws[b][:, k, :], 1.0, raws[b][:, k, :], MULT, MULT, accum_out=sumsq[:, i : i + 1]
+                    )
+                else:
+                    nc.scalar.activation(squares[:], raws[b][:, k, :], SQUARE, accum_out=sumsq[:, i : i + 1])
             nc.scalar.activation(excess, sumsq, RELU, bias=minus_floor[:])
             nc.scalar.activation(inverse, excess, RSQRT, bias=floor[:])
             cn = work.tile([P, PAIR, D], BF16, name="cn")
-            for i, k in enumerate(pair):
+            for i, (b, k) in enumerate(step):
                 scaled(b, cn[:, i, :], raws[b][:, k, :], inverse[:, i : i + 1])
             flipped = flip_banks.tile([P, PAIR, HALVES, P], BF16, name="flipped")
             for i in range(PAIR):
                 for h in range(HALVES):
                     nc.tensor.transpose(flipped[:, i, h, :], cn[:, i, h * P : (h + 1) * P], identity[:])
-            cn_t = ahead.tile([P, PAIR, HALVES, P], BF16, name="cn_t")
-            moved(b, cn_t[:], flipped[:])
+            cn_t = work.tile([P, PAIR, HALVES, P], BF16, name="cn_t")
+            moved(step[0][0], cn_t[:], flipped[:])
             return cn_t
 
-        cn_ts = []
+        def similarities(cn_t):
+            sims = []
+            for i in range(PAIR):
+                sim = sim_banks.tile([P, N], F32, name="sim")
+                for h in range(HALVES):
+                    nc.tensor.matmul(
+                        sim[:], cn_t[:, i, h, :], codes_sb[:, h, :], start=(h == 0), stop=(h == HALVES - 1)
+                    )
+                sims.append(sim)
+            return sims
 
-        def normalise_block(b):
-            cn_ts.append([normalise_and_flip(b, range(first, first + PAIR)) for first in range(0, K, PAIR)])
+        def parts(b):
+            return [slice(0, N // 2), slice(N // 2, N)] if b < ALONE else [slice(0, N)]
 
-        def similarity(b, k):
-            sim = sim_banks.tile([P, N], F32, name="sim")
-            for h in range(HALVES):
-                nc.tensor.matmul(
-                    sim[:], cn_ts[b][k // PAIR][:, k % PAIR, h, :], codes_sb[:, h, :],
-                    start=(h == 0), stop=(h == HALVES - 1),
-                )
-            return sim
-
-        for b in range(LEAD):
-            normalise_block(b)
         bests = []
-        negateds = []
-        for t in range(BLOCKS + 2):
-            if t < BLOCKS:
-                best = work.tile([P, N], F32, name="best")
-                bests.append(best)
-                moved(t, best[:], similarity(t, 0)[:])
-                nc.vector.tensor_max(best[:], best[:], similarity(t, 1)[:])
-            if 1 <= t <= BLOCKS:
-                nc.vector.tensor_max(bests[t - 1][:], bests[t - 1][:], similarity(t - 1, 3)[:])
-            if t < BLOCKS:
-                nc.vector.tensor_max(best[:], best[:], similarity(t, 2)[:])
-            if 1 <= t <= BLOCKS:
-                negated = work.tile([P, N], F32, name="negated")
-                negateds.append(negated)
-                nc.vector.tensor_scalar_mul(negated[:], bests[t - 1][:], -1.0)
-            if t >= 2:
-                nc.vector.tensor_tensor(windows[t - 2][:].indirect(offsets[:]), ones[:], negateds[t - 2][:], ADD)
-                nc.sync.dma_start(out_blocks[t - 2, :, :], windows[t - 2][:])
-            if t + LEAD < BLOCKS:
-                normalise_block(t + LEAD)
+        for step in steps:
+            sims = similarities(normalise_and_flip(step))
+            for (b, k), sim in zip(step, sims):
+                if k == 0:
+                    bests.append(work.tile([P, N], F32, name="best"))
+                for part in parts(b):
+                    if k == 0:
+                        moved(b, bests[b][:, part], sim[:, part])
+                    else:
+                        nc.vector.tensor_max(bests[b][:, part], bests[b][:, part], sim[:, part])
+            scored = [b for b, k in step if k == K - 1]
+            negateds = [work.tile([P, N], F32, name="negated") for b in scored]
+            for b, negated in zip(scored, negateds):
+                for part in parts(b):
+                    nc.vector.tensor_scalar_mul(negated[:, part], bests[b][:, part], -1.0)
+            for b, negated in zip(scored, negateds):
+                nc.vector.tensor_tensor(windows[b][:].indirect(offsets[:]), ones[:], negated[:], ADD)
+                nc.sync.dma_start(out_blocks[b, :, :], windows[b][:])

@@ -100,7 +100,7 @@ def tile_osrsaf_trinet_kernel(tc, base, codes, centroids, offs, out):
             flipped = flip_banks.tile([P, PAIR, HALVES, P], BF16, name="flipped")
             for i in range(PAIR):
                 for h in range(HALVES):
-                    nc.tensor.transpose(flipped[:, i, h, :], cn[:, i, h * P : (h + 1) * P], identity[:])
+                    nc.tensor.matmul(flipped[:, i, h, :], cn[:, i, h * P : (h + 1) * P], identity[:])
             cn_t = work.tile([P, PAIR, HALVES, P], BF16, name="cn_t")
             moved(step[0][0], cn_t[:], flipped[:])
             return cn_t

@@ -60,12 +60,14 @@ def tile_osrsaf_trinet_kernel(tc, base, codes, centroids, offs, out):
         for b in groups[-1]:
             nc.sync.dma_start(windows[b][:], base_blocks[b, :, :])
 
+        floor = held.tile([P, 1], F32, name="floor")
+        nc.gpsimd.memset(floor[:], EPS * EPS)
+        warmed = held.tile([P, 1], F32, name="warmed")
+        nc.scalar.activation(warmed[:], floor[:], RSQRT)
         identity = held.tile([P, P], BF16, name="identity")
         make_identity(nc, identity[:])
         ones = held.tile([P, N], F32, name="ones")
         nc.gpsimd.memset(ones[:], 1.0)
-        floor = held.tile([P, 1], F32, name="floor")
-        nc.gpsimd.memset(floor[:], EPS * EPS)
         minus_floor = held.tile([P, 1], F32, name="minus_floor")
         nc.gpsimd.memset(minus_floor[:], -EPS * EPS)
 

@@ -21,6 +21,7 @@ FLOPS = 2 * C * K * D * N
 PAIR = 2
 ALONE = 2
 HELPED = 1
+WARMING = 6
 
 
 def tile_osrsaf_trinet_kernel(tc, base, codes, centroids, offs, out):
@@ -68,6 +69,11 @@ def tile_osrsaf_trinet_kernel(tc, base, codes, centroids, offs, out):
         make_identity(nc, identity[:])
         ones = held.tile([P, N], F32, name="ones")
         nc.gpsimd.memset(ones[:], 1.0)
+        still = held.tile([P, N], BF16, name="still")
+        nc.vector.memset(still[:], 0.0)
+        unread = sim_banks.tile([P, N], F32, name="sim")
+        for turn in range(WARMING):
+            nc.tensor.matmul(unread[:], identity[:], still[:], start=True, stop=True)
         minus_floor = held.tile([P, 1], F32, name="minus_floor")
         nc.gpsimd.memset(minus_floor[:], -EPS * EPS)
 

import concourse.mybir as mybir
from concourse.masks import make_identity

F32 = mybir.dt.float32
BF16 = mybir.dt.bfloat16
U16 = mybir.dt.uint16
SQUARE = mybir.ActivationFunctionType.Square
RELU = mybir.ActivationFunctionType.Relu
RSQRT = mybir.ActivationFunctionType.Abs_reciprocal_sqrt
COPY = mybir.ActivationFunctionType.Copy
ADD = mybir.AluOpType.add
MULT = mybir.AluOpType.mult

P = 128
C, K, D, S, N = 1024, 4, 256, 1024, 512
BLOCKS = C // P
HALVES = D // P
EPS = 1e-12

FLOPS = 2 * C * K * D * N
PAIR = 2
ALONE = 2
HELPED = 1
WARMING = 6


def tile_osrsaf_trinet_kernel(tc, base, codes, centroids, offs, out):
    nc = tc.nc
    base_blocks = base.rearrange("(b p) s -> b p s", p=P)
    out_blocks = out.rearrange("(b p) s -> b p s", p=P)
    centroid_blocks = centroids.rearrange("(b p) k d -> b p k d", p=P)

    groups = [[b] for b in range(ALONE)] + [[b, b + 1] for b in range(ALONE, BLOCKS, 2)]
    steps = []
    for group in groups:
        units = [(b, k) for k in range(K) for b in group]
        steps.extend(units[i : i + PAIR] for i in range(0, len(units), PAIR))

    with (
        tc.tile_pool(name="held", bufs=1) as held,
        tc.tile_pool(name="inputs", bufs=BLOCKS) as inputs,
        tc.tile_pool(name="lengths", bufs=2) as lengths,
        tc.tile_pool(name="work", bufs=4) as work,
        tc.psum_pool(name="flip_banks", bufs=2) as flip_banks,
        tc.psum_pool(name="sim_banks", bufs=6) as sim_banks,
    ):
        raws = [inputs.tile([P, K, D], F32, name="raw") for b in range(BLOCKS)]
        windows = [inputs.tile([P, S], F32, name="window") for b in range(BLOCKS)]
        codes_sb = held.tile([P, HALVES, N], BF16, name="codes_sb")
        offsets = held.tile([P, N // 16], U16, name="offsets")
        for g, group in enumerate(groups):
            for k in range(K):
                for b in group:
                    nc.sync.dma_start(raws[b][:, k, :], centroid_blocks[b, :, k, :])
            if g == 0:
                nc.sync.dma_start(codes_sb[:], codes.rearrange("(h p) j -> p h j", p=P))
                nc.sync.dma_start(offsets[:], offs)
            else:
                for b in groups[g - 1]:
                    nc.sync.dma_start(windows[b][:], base_blocks[b, :, :])
        for b in groups[-1]:
            nc.sync.dma_start(windows[b][:], base_blocks[b, :, :])

        floor = held.tile([P, 1], F32, name="floor")
        nc.gpsimd.memset(floor[:], EPS * EPS)
        warmed = held.tile([P, 1], F32, name="warmed")
        nc.scalar.activation(warmed[:], floor[:], RSQRT)
        identity = held.tile([P, P], BF16, name="identity")
        make_identity(nc, identity[:])
        ones = held.tile([P, N], F32, name="ones")
        nc.gpsimd.memset(ones[:], 1.0)
        still = held.tile([P, N], BF16, name="still")
        nc.vector.memset(still[:], 0.0)
        unread = sim_banks.tile([P, N], F32, name="sim")
        for turn in range(WARMING):
            nc.tensor.matmul(unread[:], identity[:], still[:], start=True, stop=True)
        minus_floor = held.tile([P, 1], F32, name="minus_floor")
        nc.gpsimd.memset(minus_floor[:], -EPS * EPS)

        def scaled(b, result, values, factor):
            if b < HELPED:
                nc.vector.tensor_scalar_mul(result, values, factor)
            else:
                nc.scalar.activation(result, values, COPY, scale=factor)

        def moved(b, result, values):
            if b < HELPED:
                nc.vector.tensor_copy(result, values)
            else:
                nc.scalar.copy(result, values)

        def normalise_and_flip(step):
            small = lengths.tile([P, 3, PAIR], F32, name="small")
            sumsq, excess, inverse = small[:, 0, :], small[:, 1, :], small[:, 2, :]
            for i, (b, k) in enumerate(step):
                squares = work.tile([P, D], F32, name="squares")
                if b < HELPED and k >= PAIR:
                    nc.vector.scalar_tensor_tensor(
                        squares[:], raws[b][:, k, :], 1.0, raws[b][:, k, :], MULT, MULT, accum_out=sumsq[:, i : i + 1]
                    )
                else:
                    nc.scalar.activation(squares[:], raws[b][:, k, :], SQUARE, accum_out=sumsq[:, i : i + 1])
            nc.scalar.activation(excess, sumsq, RELU, bias=minus_floor[:])
            nc.scalar.activation(inverse, excess, RSQRT, bias=floor[:])
            cn = work.tile([P, PAIR, D], BF16, name="cn")
            for i, (b, k) in enumerate(step):
                scaled(b, cn[:, i, :], raws[b][:, k, :], inverse[:, i : i + 1])
            flipped = flip_banks.tile([P, PAIR, HALVES, P], BF16, name="flipped")
            for i in range(PAIR):
                for h in range(HALVES):
                    nc.tensor.matmul(flipped[:, i, h, :], cn[:, i, h * P : (h + 1) * P], identity[:])
            cn_t = work.tile([P, PAIR, HALVES, P], BF16, name="cn_t")
            moved(step[0][0], cn_t[:], flipped[:])
            return cn_t

        def similarities(cn_t):
            sims = []
            for i in range(PAIR):
                sim = sim_banks.tile([P, N], F32, name="sim")
                for h in range(HALVES):
                    nc.tensor.matmul(
                        sim[:], cn_t[:, i, h, :], codes_sb[:, h, :], start=(h == 0), stop=(h == HALVES - 1)
                    )
                sims.append(sim)
            return sims

        def parts(b):
            return [slice(0, N // 2), slice(N // 2, N)] if b < ALONE else [slice(0, N)]

        bests = []
        for step in steps:
            sims = similarities(normalise_and_flip(step))
            for (b, k), sim in zip(step, sims):
                if k == 0:
                    bests.append(work.tile([P, N], F32, name="best"))
                for part in parts(b):
                    if k == 0:
                        moved(b, bests[b][:, part], sim[:, part])
                    else:
                        nc.vector.tensor_max(bests[b][:, part], bests[b][:, part], sim[:, part])
            scored = [b for b, k in step if k == K - 1]
            negateds = [work.tile([P, N], F32, name="negated") for b in scored]
            for b, negated in zip(scored, negateds):
                for part in parts(b):
                    nc.vector.tensor_scalar_mul(negated[:, part], bests[b][:, part], -1.0)
            for b, negated in zip(scored, negateds):
                nc.vector.tensor_tensor(windows[b][:].indirect(offsets[:]), ones[:], negated[:], ADD)
                nc.sync.dma_start(out_blocks[b, :, :], windows[b][:])
